import numpy as np
import ml_dtypes


def mxq(x, axis, fmt="e4m3"):
    dtype, down = {"e4m3": (ml_dtypes.float8_e4m3fn, 7), "e5m2": (ml_dtypes.float8_e5m2, 14)}[fmt]
    v = np.moveaxis(np.asarray(x, np.float32).astype(ml_dtypes.bfloat16).astype(np.float64), axis, -1)
    blocks = v.reshape(v.shape[:-1] + (-1, 32))
    amax = np.abs(blocks).max(-1, keepdims=True)
    byte = np.maximum(np.where(amax > 0, np.frexp(amax)[1] - 1 + 127, 0) - down, 1)
    scale = np.exp2(byte - 127.0)
    codes = (blocks / scale).astype(np.float32).astype(dtype).astype(np.float64)
    return np.moveaxis((codes * scale).reshape(v.shape), -1, axis)


WIDE = False


def mx_kscale(k):
    if not WIDE:
        return np.ones(k)
    levels = np.array([10, -10, 5, -5, 0])
    a = np.random.permutation(np.resize(levels, k // 512 * 4)).reshape(k // 512, 4)
    idx = np.arange(k)
    return np.exp2(a[idx // 512, idx % 128 // 32])


BF16 = ml_dtypes.bfloat16


def bf(x):
    return np.asarray(x, np.float32).astype(BF16)


def f64(x):
    return np.asarray(x).astype(np.float64)


N, V, EN1, EN2, D, K, EMB = 256, 4096, 1024, 512, 128, 512, 1024
BN_EPS = 1e-5


def batchnorm(x):
    m = x.mean(axis=0)
    v = x.var(axis=0)
    return (x - m) * (1.0 / np.sqrt(v + BN_EPS))


def setup_inputs():
    s, t = mx_kscale(EN1), mx_kscale(EN2)
    return {
        "en1": bf(np.maximum(np.random.standard_normal((N, EN1)) * 1.15, 0.0) * s),
        "W2": bf(np.random.standard_normal((EN1, EN2)) / np.sqrt(EN1) / s[:, None] * t),
        "b2": bf(np.random.standard_normal(EN2) * 0.2 * t),
        "Wmean": bf(np.random.standard_normal((EN2, D)) / np.sqrt(EN2) / t[:, None]),
        "Wlogvar": bf(np.random.standard_normal((EN2, D)) / np.sqrt(EN2) / t[:, None]),
        "eps": bf(np.random.standard_normal((N, D))),
    }


def reference(en1, W2, b2, Wmean, Wlogvar, eps):
    en2 = np.maximum((mxq(f64(en1), 1, "e4m3") @ mxq(f64(W2), 0, "e4m3")) + f64(b2), 0.0)
    en2q = mxq(en2, 1, "e4m3")
    posterior_mean = batchnorm(en2q @ mxq(f64(Wmean), 0, "e4m3"))
    posterior_logvar = batchnorm(en2q @ mxq(f64(Wlogvar), 0, "e4m3"))
    posterior_var = np.exp(posterior_logvar)
    z = posterior_mean + np.sqrt(posterior_var) * f64(eps)
    zx = batchnorm(z)
    return z, zx

@@ -1,0 +1,196 @@
+from contextlib import ExitStack
+
+import concourse.mybir as mybir
+from concourse.masks import make_identity
+
+F32 = mybir.dt.float32
+BF16 = mybir.dt.bfloat16
+U32 = mybir.dt.uint32
+U8 = mybir.dt.uint8
+FP8X4 = mybir.dt.float8_e4m3fn_x4
+ALU = mybir.AluOpType
+ACT = mybir.ActivationFunctionType
+
+P = 128
+PACK = 4
+K_PASS = P * PACK
+ROWS = 256
+EN1 = 1024
+EN2 = 512
+D = 128
+ROW_TILES = ROWS // P
+PASSES_1 = EN1 // K_PASS
+BN_EPS = 1e-5
+
+VECTOR_COLS = 80
+
+FLOPS = 2 * ROWS * EN1 * EN2 + 2 * 2 * ROWS * EN2 * D
+
+
+def column_stats(nc, pool, values, mean_var):
+    stats = pool.tile([P, 6], F32, name="stats")
+    nc.vector.bn_stats(out=stats[:], in_=values)
+    nc.vector.bn_aggr(out=mean_var, in_=stats[:])
+
+
+def tile_modelvd_pa_s_kernel(tc, en1, W2, b2, Wmean, Wlogvar, eps, out_0, out_1):
+    nc = tc.nc
+    with ExitStack() as stack:
+        keep = stack.enter_context(tc.tile_pool(name="keep", bufs=1))
+        small = stack.enter_context(tc.tile_pool(name="small", bufs=4))
+        psum = stack.enter_context(tc.psum_pool(name="psum", bufs=1))
+
+        ident_f32 = keep.tile([P, P], F32)
+        make_identity(nc, ident_f32[:])
+        ident_bf16 = keep.tile([P, P], BF16)
+        make_identity(nc, ident_bf16[:])
+        neg_half = keep.tile([P, 2], F32)
+        nc.vector.memset(neg_half[:], -0.5)
+        warm_in = keep.tile([P, 1], F32)
+        warm_out = keep.tile([P, 1], F32)
+        nc.vector.memset(warm_in[:], 0.0)
+        nc.scalar.activation(out=warm_out[:], in_=warm_in[:], func=ACT.Exp)
+
+        x_sb = [keep.tile([P, EN1], BF16, name="x_sb%d" % r) for r in range(ROW_TILES)]
+        for r in range(ROW_TILES):
+            nc.sync.dma_start(out=x_sb[r][:], in_=en1[r * P : (r + 1) * P, :])
+        w_raw = [keep.tile([P, PACK, EN2], BF16, name="w_raw%d" % g) for g in range(PASSES_1)]
+        for g in range(PASSES_1):
+            nc.sync.dma_start(
+                out=w_raw[g][:],
+                in_=W2[g * K_PASS : (g + 1) * K_PASS, :].rearrange("(p t) n -> p t n", t=PACK),
+            )
+        head_raw = keep.tile([P, 2, PACK, D], BF16)
+        nc.sync.dma_start(out=head_raw[:, 0], in_=Wmean.rearrange("(p t) d -> p t d", t=PACK))
+        nc.sync.dma_start(out=head_raw[:, 1], in_=Wlogvar.rearrange("(p t) d -> p t d", t=PACK))
+        eps_sb = keep.tile([P, ROW_TILES, D], BF16)
+        nc.sync.dma_start(out=eps_sb[:], in_=eps.rearrange("(r p) d -> p r d", p=P))
+        b2_bf = keep.tile([P, PACK], BF16)
+        nc.scalar.dma_start(out=b2_bf[:], in_=b2.rearrange("(p j) -> p j", j=PACK))
+        b2_f32 = keep.tile([P, PACK], F32)
+        nc.gpsimd.tensor_copy(out=b2_f32[:], in_=b2_bf[:])
+
+        x_grouped = keep.tile([P, PASSES_1, ROWS * PACK], BF16, align_bytes=64)
+        x_codes = keep.tile([P, PASSES_1, ROWS], U32, align_bytes=64)
+        x_scales = keep.tile([P, PASSES_1, ROWS], U8, align_bytes=64)
+        for g in range(PASSES_1):
+            x_t = psum.tile([P, 2, ROWS], F32, name="x_t%d" % g, tag="early%d" % g)
+            for u in range(2):
+                for r in range(ROW_TILES):
+                    words = x_sb[r][:].bitcast(F32).rearrange("p (g w u) -> p g u w", g=PASSES_1, u=2)
+                    nc.tensor.transpose(x_t[:, u, r * P : (r + 1) * P], words[:, g, u, :], ident_f32[:])
+            nc.scalar.copy(
+                out=x_grouped[:, g, :].bitcast(F32).rearrange("p (r u) -> p r u", u=2),
+                in_=x_t[:].rearrange("p u r -> p r u"),
+            )
+        for g in range(PASSES_1):
+            nc.vector.quantize_mx(
+                out=x_codes[:, g, :].bitcast(FP8X4), scales=x_scales[:, g, :], in_=x_grouped[:, g, :]
+            )
+
+        w_codes = [keep.tile([P, EN2], U32, name="w_codes%d" % g, align_bytes=64) for g in range(PASSES_1)]
+        w_scales = [keep.tile([P, EN2], U8, name="w_scales%d" % g, align_bytes=64) for g in range(PASSES_1)]
+        for g in range(PASSES_1):
+            w_grouped = keep.tile([P, EN2 * PACK], BF16, name="w_grouped%d" % g, align_bytes=64)
+            dst = w_grouped[:].rearrange("p (j m t) -> p m t j", j=PACK, t=PACK)
+            src = w_raw[g][:].rearrange("p t (m j) -> p m t j", j=PACK)
+            nc.vector.tensor_copy(out=dst[:, :VECTOR_COLS], in_=src[:, :VECTOR_COLS])
+            nc.scalar.copy(out=dst[:, VECTOR_COLS:], in_=src[:, VECTOR_COLS:])
+            nc.vector.quantize_mx(out=w_codes[g][:].bitcast(FP8X4), scales=w_scales[g][:], in_=w_grouped[:])
+
+        h_ps = [psum.tile([P, ROWS], F32, name="h_ps%d" % j, tag="h%d" % j) for j in range(PACK)]
+        for g in range(PASSES_1):
+            for j in range(PACK):
+                nc.tensor.matmul_mx(
+                    out=h_ps[j][:],
+                    lhsT=w_codes[g][:, j * P : (j + 1) * P].bitcast(FP8X4),
+                    lhsT_scale=w_scales[g][:, j * P : (j + 1) * P],
+                    rhs=x_codes[:, g, :].bitcast(FP8X4),
+                    rhs_scale=x_scales[:, g, :],
+                    start=(g == 0),
+                    stop=(g == PASSES_1 - 1),
+                )
+
+        head_grouped = keep.tile([P, 2 * D * PACK], BF16, align_bytes=64)
+        head_codes = keep.tile([P, 2 * D], U32, align_bytes=64)
+        head_scales = keep.tile([P, 2 * D], U8, align_bytes=64)
+        nc.scalar.copy(
+            out=head_grouped[:].rearrange("p (w d t) -> p w d t", w=2, t=PACK),
+            in_=head_raw[:].rearrange("p w t d -> p w d t"),
+        )
+        nc.vector.quantize_mx(out=head_codes[:].bitcast(FP8X4), scales=head_scales[:], in_=head_grouped[:])
+        eps_t = psum.tile([P, ROWS], BF16, tag="eps")
+        for r in range(ROW_TILES):
+            nc.tensor.transpose(eps_t[:, r * P : (r + 1) * P], eps_sb[:, r, :], ident_bf16[:])
+
+        h_bf = keep.tile([P, PACK, ROWS], BF16)
+        for j in range(PACK):
+            if j % 2 == 0:
+                nc.scalar.activation(out=h_bf[:, j, :], in_=h_ps[j][:], func=ACT.Relu, bias=b2_f32[:, j : j + 1])
+            else:
+                nc.vector.tensor_scalar(
+                    out=h_bf[:, j, :], in0=h_ps[j][:], scalar1=b2_f32[:, j : j + 1], scalar2=0.0,
+                    op0=ALU.add, op1=ALU.max,
+                )
+        h_grouped = keep.tile([P, ROWS * PACK], BF16, align_bytes=64)
+        h_codes = keep.tile([P, ROWS], U32, align_bytes=64)
+        h_scales = keep.tile([P, ROWS], U8, align_bytes=64)
+        nc.vector.tensor_copy(
+            out=h_grouped[:].rearrange("p (r t) -> p r t", t=PACK), in_=h_bf[:].rearrange("p t r -> p r t")
+        )
+        nc.vector.quantize_mx(out=h_codes[:].bitcast(FP8X4), scales=h_scales[:], in_=h_grouped[:])
+
+        head_ps = [psum.tile([P, ROWS], F32, name="head_ps%d" % w, tag="early%d" % w) for w in range(2)]
+        for w in range(2):
+            nc.tensor.matmul_mx(
+                out=head_ps[w][:],
+                lhsT=head_codes[:, w * D : (w + 1) * D].bitcast(FP8X4),
+                lhsT_scale=head_scales[:, w * D : (w + 1) * D],
+                rhs=h_codes[:].bitcast(FP8X4),
+                rhs_scale=h_scales[:],
+                start=True,
+                stop=True,
+            )
+        m_ps, lv_ps = head_ps
+
+        mean_var = keep.tile([P, 2, 2], F32)
+        for w in range(2):
+            column_stats(nc, small, head_ps[w][:], mean_var[:, w, :])
+        var_eps = keep.tile([P, 2], F32)
+        nc.vector.tensor_scalar_add(out=var_eps[:], in0=mean_var[:, :, 1], scalar1=BN_EPS)
+        rstd = keep.tile([P, 2], F32)
+        nc.gpsimd.tensor_tensor(out=rstd[:], in0=var_eps[:], in1=neg_half[:], op=ALU.pow)
+        lv_half = keep.tile([P, ROWS], F32)
+        nc.vector.tensor_scalar(
+            out=lv_half[:], in0=lv_ps[:], scalar1=mean_var[:, 1, 0:1], scalar2=0.5, op0=ALU.subtract, op1=ALU.mult
+        )
+        m_centred = keep.tile([P, ROWS], F32)
+        nc.vector.tensor_scalar_sub(out=m_centred[:], in0=m_ps[:], scalar1=mean_var[:, 0, 0:1])
+        std_dev = keep.tile([P, ROWS], F32)
+        nc.scalar.activation(out=std_dev[:], in_=lv_half[:], func=ACT.Exp, scale=rstd[:, 1:2])
+        noise = keep.tile([P, ROWS], F32)
+        nc.vector.tensor_tensor(out=noise[:], in0=std_dev[:], in1=eps_t[:], op=ALU.mult)
+        z_t = keep.tile([P, ROWS], F32)
+        nc.vector.scalar_tensor_tensor(
+            out=z_t[:], in0=m_centred[:], scalar=rstd[:, 0:1], in1=noise[:], op0=ALU.mult, op1=ALU.add
+        )
+
+        z_mean_var = keep.tile([P, 2], F32)
+        column_stats(nc, small, z_t[:], z_mean_var[:])
+        z_var_eps = keep.tile([P, 1], F32)
+        nc.vector.tensor_scalar_add(out=z_var_eps[:], in0=z_mean_var[:, 1:2], scalar1=BN_EPS)
+        z_rstd = keep.tile([P, 1], F32)
+        nc.gpsimd.tensor_tensor(out=z_rstd[:], in0=z_var_eps[:], in1=neg_half[:, 0:1], op=ALU.pow)
+        zx_t = keep.tile([P, ROWS], F32)
+        nc.vector.tensor_scalar(
+            out=zx_t[:], in0=z_t[:], scalar1=z_mean_var[:, 0:1], scalar2=z_rstd[:, 0:1],
+            op0=ALU.subtract, op1=ALU.mult,
+        )
+
+        for index, (result_t, out) in enumerate(((z_t, out_0), (zx_t, out_1))):
+            back_ps = psum.tile([P, ROW_TILES, D], F32, name="back_ps%d" % index, tag="h%d" % index)
+            for r in range(ROW_TILES):
+                nc.tensor.transpose(back_ps[:, r, :], result_t[:, r * P : (r + 1) * P], ident_f32[:])
+            result = keep.tile([P, ROW_TILES, D], F32, name="result%d" % index)
+            nc.scalar.copy(out=result[:], in_=back_ps[:])
+            nc.sync.dma_start(out=out.rearrange("(r p) d -> p r d", p=P), in_=result[:])

@@ -22,84 +22,104 @@ ROW_TILES = ROWS // P
 PASSES_1 = EN1 // K_PASS
 BN_EPS = 1e-5
 
-VECTOR_COLS = 80
+HALF = EN2 // 2
+
+VECTOR_COLS = 64
+VECTOR_ROWS = 168
 
 FLOPS = 2 * ROWS * EN1 * EN2 + 2 * 2 * ROWS * EN2 * D
-
-
-def column_stats(nc, pool, values, mean_var):
-    stats = pool.tile([P, 6], F32, name="stats")
-    nc.vector.bn_stats(out=stats[:], in_=values)
-    nc.vector.bn_aggr(out=mean_var, in_=stats[:])
 
 
 def tile_modelvd_pa_s_kernel(tc, en1, W2, b2, Wmean, Wlogvar, eps, out_0, out_1):
     nc = tc.nc
     with ExitStack() as stack:
         keep = stack.enter_context(tc.tile_pool(name="keep", bufs=1))
-        small = stack.enter_context(tc.tile_pool(name="small", bufs=4))
         psum = stack.enter_context(tc.psum_pool(name="psum", bufs=1))
+        stack.enter_context(tc.manual_schedule())
 
         ident_f32 = keep.tile([P, P], F32)
         make_identity(nc, ident_f32[:])
         ident_bf16 = keep.tile([P, P], BF16)
         make_identity(nc, ident_bf16[:])
-        neg_half = keep.tile([P, 2], F32)
+        neg_half = keep.tile([P, 1], F32)
         nc.vector.memset(neg_half[:], -0.5)
-        warm_in = keep.tile([P, 1], F32)
-        warm_out = keep.tile([P, 1], F32)
-        nc.vector.memset(warm_in[:], 0.0)
-        nc.scalar.activation(out=warm_out[:], in_=warm_in[:], func=ACT.Exp)
+        bn_eps = keep.tile([P, 1], F32)
+        nc.vector.memset(bn_eps[:], BN_EPS)
+        one = keep.tile([P, 1], F32)
+        nc.vector.memset(one[:], 1.0)
 
         x_sb = [keep.tile([P, EN1], BF16, name="x_sb%d" % r) for r in range(ROW_TILES)]
-        for r in range(ROW_TILES):
-            nc.sync.dma_start(out=x_sb[r][:], in_=en1[r * P : (r + 1) * P, :])
         w_raw = [keep.tile([P, PACK, EN2], BF16, name="w_raw%d" % g) for g in range(PASSES_1)]
-        for g in range(PASSES_1):
+
+        def load_x(r):
+            nc.sync.dma_start(out=x_sb[r][:], in_=en1[r * P : (r + 1) * P, :])
+
+        def load_w(g):
             nc.sync.dma_start(
-                out=w_raw[g][:],
-                in_=W2[g * K_PASS : (g + 1) * K_PASS, :].rearrange("(p t) n -> p t n", t=PACK),
+                out=w_raw[g][:].rearrange("p (u e) n -> p u (e n)", u=2),
+                in_=W2[g * K_PASS : (g + 1) * K_PASS, :].rearrange("(u p e) n -> p u (e n)", u=2, e=2),
             )
+
+        load_x(0)
+        load_x(1)
+        load_w(0)
+        load_w(1)
         head_raw = keep.tile([P, 2, PACK, D], BF16)
-        nc.sync.dma_start(out=head_raw[:, 0], in_=Wmean.rearrange("(p t) d -> p t d", t=PACK))
-        nc.sync.dma_start(out=head_raw[:, 1], in_=Wlogvar.rearrange("(p t) d -> p t d", t=PACK))
+        nc.sync.dma_start(out=head_raw[:, 0], in_=Wlogvar.rearrange("(p t) d -> p t d", t=PACK))
+        nc.sync.dma_start(out=head_raw[:, 1], in_=Wmean.rearrange("(p t) d -> p t d", t=PACK))
         eps_sb = keep.tile([P, ROW_TILES, D], BF16)
         nc.sync.dma_start(out=eps_sb[:], in_=eps.rearrange("(r p) d -> p r d", p=P))
         b2_bf = keep.tile([P, PACK], BF16)
         nc.scalar.dma_start(out=b2_bf[:], in_=b2.rearrange("(p j) -> p j", j=PACK))
         b2_f32 = keep.tile([P, PACK], F32)
         nc.gpsimd.tensor_copy(out=b2_f32[:], in_=b2_bf[:])
+        warm = keep.tile([P, 1], F32)
+        nc.scalar.activation(out=warm[:], in_=one[:], func=ACT.Exp)
 
         x_grouped = keep.tile([P, PASSES_1, ROWS * PACK], BF16, align_bytes=64)
         x_codes = keep.tile([P, PASSES_1, ROWS], U32, align_bytes=64)
         x_scales = keep.tile([P, PASSES_1, ROWS], U8, align_bytes=64)
-        for g in range(PASSES_1):
-            x_t = psum.tile([P, 2, ROWS], F32, name="x_t%d" % g, tag="early%d" % g)
-            for u in range(2):
-                for r in range(ROW_TILES):
-                    words = x_sb[r][:].bitcast(F32).rearrange("p (g w u) -> p g u w", g=PASSES_1, u=2)
-                    nc.tensor.transpose(x_t[:, u, r * P : (r + 1) * P], words[:, g, u, :], ident_f32[:])
+
+        def transpose_x(r):
+            x_t = psum.tile([P, PASSES_1, 2, P], F32, name="x_t%d" % r, tag="early%d" % r)
+            words = x_sb[r][:].bitcast(F32).rearrange("p (g u w) -> p g u w", g=PASSES_1, u=2)
+            for g in range(PASSES_1):
+                for u in range(2):
+                    nc.tensor.transpose(x_t[:, g, u, :], words[:, g, u, :], ident_f32[:])
+            grouped_words = x_grouped[:].bitcast(F32).rearrange("p g (r u) -> p g r u", u=2)
             nc.scalar.copy(
-                out=x_grouped[:, g, :].bitcast(F32).rearrange("p (r u) -> p r u", u=2),
-                in_=x_t[:].rearrange("p u r -> p r u"),
-            )
-        for g in range(PASSES_1):
-            nc.vector.quantize_mx(
-                out=x_codes[:, g, :].bitcast(FP8X4), scales=x_scales[:, g, :], in_=x_grouped[:, g, :]
+                out=grouped_words[:, :, r * P : (r + 1) * P, :], in_=x_t[:].rearrange("p g u r -> p g r u")
             )
 
+        def quantise_x(r):
+            for g in range(PASSES_1):
+                nc.vector.quantize_mx(
+                    out=x_codes[:, g, r * P : (r + 1) * P].bitcast(FP8X4),
+                    scales=x_scales[:, g, r * P : (r + 1) * P],
+                    in_=x_grouped[:, g, r * P * PACK : (r + 1) * P * PACK],
+                )
+
+        w_grouped = [keep.tile([P, EN2 * PACK], BF16, name="w_grouped%d" % g, align_bytes=64) for g in range(PASSES_1)]
         w_codes = [keep.tile([P, EN2], U32, name="w_codes%d" % g, align_bytes=64) for g in range(PASSES_1)]
         w_scales = [keep.tile([P, EN2], U8, name="w_scales%d" % g, align_bytes=64) for g in range(PASSES_1)]
-        for g in range(PASSES_1):
-            w_grouped = keep.tile([P, EN2 * PACK], BF16, name="w_grouped%d" % g, align_bytes=64)
-            dst = w_grouped[:].rearrange("p (j m t) -> p m t j", j=PACK, t=PACK)
+
+        def regroup_w(g, half):
+            blocks = slice(2 * half, 2 * half + 2)
+            dst = w_grouped[g][:].rearrange("p (j m t) -> p m t j", j=PACK, t=PACK)
             src = w_raw[g][:].rearrange("p t (m j) -> p m t j", j=PACK)
-            nc.vector.tensor_copy(out=dst[:, :VECTOR_COLS], in_=src[:, :VECTOR_COLS])
-            nc.scalar.copy(out=dst[:, VECTOR_COLS:], in_=src[:, VECTOR_COLS:])
-            nc.vector.quantize_mx(out=w_codes[g][:].bitcast(FP8X4), scales=w_scales[g][:], in_=w_grouped[:])
+            nc.vector.tensor_copy(out=dst[:, :VECTOR_COLS, :, blocks], in_=src[:, :VECTOR_COLS, :, blocks])
+            nc.scalar.copy(out=dst[:, VECTOR_COLS:, :, blocks], in_=src[:, VECTOR_COLS:, :, blocks])
+
+        def quantise_w(g, half):
+            nc.vector.quantize_mx(
+                out=w_codes[g][:, half * HALF : (half + 1) * HALF].bitcast(FP8X4),
+                scales=w_scales[g][:, half * HALF : (half + 1) * HALF],
+                in_=w_grouped[g][:, half * HALF * PACK : (half + 1) * HALF * PACK],
+            )
 
         h_ps = [psum.tile([P, ROWS], F32, name="h_ps%d" % j, tag="h%d" % j) for j in range(PACK)]
-        for g in range(PASSES_1):
+
+        def multiply_1(g):
             for j in range(PACK):
                 nc.tensor.matmul_mx(
                     out=h_ps[j][:],
@@ -111,13 +131,28 @@ def tile_modelvd_pa_s_kernel(tc, en1, W2, b2, Wmean, Wlogvar, eps, out_0, out_1)
                     stop=(g == PASSES_1 - 1),
                 )
 
+        transpose_x(0)
+        transpose_x(1)
+        regroup_w(0, 0)
+        regroup_w(0, 1)
+        quantise_x(0)
+        quantise_w(0, 0)
+        quantise_w(0, 1)
+        quantise_x(1)
+        multiply_1(0)
+        regroup_w(1, 0)
+        regroup_w(1, 1)
+        quantise_w(1, 0)
+        quantise_w(1, 1)
+        multiply_1(1)
+
         head_grouped = keep.tile([P, 2 * D * PACK], BF16, align_bytes=64)
         head_codes = keep.tile([P, 2 * D], U32, align_bytes=64)
         head_scales = keep.tile([P, 2 * D], U8, align_bytes=64)
-        nc.scalar.copy(
-            out=head_grouped[:].rearrange("p (w d t) -> p w d t", w=2, t=PACK),
-            in_=head_raw[:].rearrange("p w t d -> p w d t"),
-        )
+        head_dst = head_grouped[:].rearrange("p (w d t) -> p w d t", w=2, t=PACK)
+        head_src = head_raw[:].rearrange("p w t d -> p w d t")
+        nc.vector.tensor_copy(out=head_dst[:, 0], in_=head_src[:, 0])
+        nc.scalar.copy(out=head_dst[:, 1], in_=head_src[:, 1])
         nc.vector.quantize_mx(out=head_codes[:].bitcast(FP8X4), scales=head_scales[:], in_=head_grouped[:])
         eps_t = psum.tile([P, ROWS], BF16, tag="eps")
         for r in range(ROW_TILES):
@@ -135,9 +170,10 @@ def tile_modelvd_pa_s_kernel(tc, en1, W2, b2, Wmean, Wlogvar, eps, out_0, out_1)
         h_grouped = keep.tile([P, ROWS * PACK], BF16, align_bytes=64)
         h_codes = keep.tile([P, ROWS], U32, align_bytes=64)
         h_scales = keep.tile([P, ROWS], U8, align_bytes=64)
-        nc.vector.tensor_copy(
-            out=h_grouped[:].rearrange("p (r t) -> p r t", t=PACK), in_=h_bf[:].rearrange("p t r -> p r t")
-        )
+        h_dst = h_grouped[:].rearrange("p (r t) -> p r t", t=PACK)
+        h_src = h_bf[:].rearrange("p t r -> p r t")
+        nc.vector.tensor_copy(out=h_dst[:, :VECTOR_ROWS], in_=h_src[:, :VECTOR_ROWS])
+        nc.scalar.copy(out=h_dst[:, VECTOR_ROWS:], in_=h_src[:, VECTOR_ROWS:])
         nc.vector.quantize_mx(out=h_codes[:].bitcast(FP8X4), scales=h_scales[:], in_=h_grouped[:])
 
         head_ps = [psum.tile([P, ROWS], F32, name="head_ps%d" % w, tag="early%d" % w) for w in range(2)]
@@ -151,46 +187,57 @@ def tile_modelvd_pa_s_kernel(tc, en1, W2, b2, Wmean, Wlogvar, eps, out_0, out_1)
                 start=True,
                 stop=True,
             )
-        m_ps, lv_ps = head_ps
+        lv_ps, m_ps = head_ps
 
-        mean_var = keep.tile([P, 2, 2], F32)
+        mean_var = [keep.tile([P, 2], F32, name="mean_var%d" % w) for w in range(2)]
+        var_eps = [keep.tile([P, 1], F32, name="var_eps%d" % w) for w in range(2)]
+        rstd = [keep.tile([P, 1], F32, name="rstd%d" % w) for w in range(2)]
+        stats = [keep.tile([P, 6], F32, name="stats%d" % w) for w in range(2)]
         for w in range(2):
-            column_stats(nc, small, head_ps[w][:], mean_var[:, w, :])
-        var_eps = keep.tile([P, 2], F32)
-        nc.vector.tensor_scalar_add(out=var_eps[:], in0=mean_var[:, :, 1], scalar1=BN_EPS)
-        rstd = keep.tile([P, 2], F32)
-        nc.gpsimd.tensor_tensor(out=rstd[:], in0=var_eps[:], in1=neg_half[:], op=ALU.pow)
+            nc.vector.bn_stats(out=stats[w][:], in_=head_ps[w][:])
+        for w in range(2):
+            nc.vector.bn_aggr(out=mean_var[w][:], in_=stats[w][:])
+        for w in range(2):
+            nc.vector.tensor_scalar_add(out=var_eps[w][:], in0=mean_var[w][:, 1:2], scalar1=BN_EPS)
+            nc.gpsimd.tensor_tensor(out=rstd[w][:], in0=var_eps[w][:], in1=neg_half[:], op=ALU.pow)
         lv_half = keep.tile([P, ROWS], F32)
         nc.vector.tensor_scalar(
-            out=lv_half[:], in0=lv_ps[:], scalar1=mean_var[:, 1, 0:1], scalar2=0.5, op0=ALU.subtract, op1=ALU.mult
+            out=lv_half[:], in0=lv_ps[:], scalar1=mean_var[0][:, 0:1], scalar2=0.5, op0=ALU.subtract, op1=ALU.mult
         )
         m_centred = keep.tile([P, ROWS], F32)
-        nc.vector.tensor_scalar_sub(out=m_centred[:], in0=m_ps[:], scalar1=mean_var[:, 0, 0:1])
+        nc.vector.tensor_scalar_sub(out=m_centred[:], in0=m_ps[:], scalar1=mean_var[1][:, 0:1])
         std_dev = keep.tile([P, ROWS], F32)
-        nc.scalar.activation(out=std_dev[:], in_=lv_half[:], func=ACT.Exp, scale=rstd[:, 1:2])
+        nc.scalar.activation(out=std_dev[:], in_=lv_half[:], func=ACT.Exp, scale=rstd[0][:])
+        nc.scalar.activation(out=warm[:], in_=one[:], func=ACT.Abs_reciprocal_sqrt)
         noise = keep.tile([P, ROWS], F32)
         nc.vector.tensor_tensor(out=noise[:], in0=std_dev[:], in1=eps_t[:], op=ALU.mult)
         z_t = keep.tile([P, ROWS], F32)
         nc.vector.scalar_tensor_tensor(
-            out=z_t[:], in0=m_centred[:], scalar=rstd[:, 0:1], in1=noise[:], op0=ALU.mult, op1=ALU.add
+            out=z_t[:], in0=m_centred[:], scalar=rstd[1][:], in1=noise[:], op0=ALU.mult, op1=ALU.add
         )
+
+        z_ps = psum.tile([P, ROW_TILES, D], F32, tag="h0")
+        for r in range(ROW_TILES):
+            nc.tensor.transpose(z_ps[:, r, :], z_t[:, r * P : (r + 1) * P], ident_f32[:])
+        z_rows = keep.tile([P, ROW_TILES, D], F32)
+        nc.scalar.copy(out=z_rows[:], in_=z_ps[:])
+        nc.sync.dma_start(out=out_0.rearrange("(r p) d -> p r d", p=P), in_=z_rows[:])
 
         z_mean_var = keep.tile([P, 2], F32)
-        column_stats(nc, small, z_t[:], z_mean_var[:])
-        z_var_eps = keep.tile([P, 1], F32)
-        nc.vector.tensor_scalar_add(out=z_var_eps[:], in0=z_mean_var[:, 1:2], scalar1=BN_EPS)
+        z_stats = keep.tile([P, 6], F32)
+        nc.vector.bn_stats(out=z_stats[:], in_=z_t[:])
+        nc.vector.bn_aggr(out=z_mean_var[:], in_=z_stats[:])
         z_rstd = keep.tile([P, 1], F32)
-        nc.gpsimd.tensor_tensor(out=z_rstd[:], in0=z_var_eps[:], in1=neg_half[:, 0:1], op=ALU.pow)
-        zx_t = keep.tile([P, ROWS], F32)
-        nc.vector.tensor_scalar(
-            out=zx_t[:], in0=z_t[:], scalar1=z_mean_var[:, 0:1], scalar2=z_rstd[:, 0:1],
-            op0=ALU.subtract, op1=ALU.mult,
+        nc.scalar.activation(out=z_rstd[:], in_=z_mean_var[:, 1:2], func=ACT.Abs_reciprocal_sqrt, bias=bn_eps[:])
+        mean_ps = psum.tile([P, D], F32, tag="h1")
+        nc.tensor.matmul(out=mean_ps[:], lhsT=z_mean_var[:, 0:1].to_broadcast([P, P]), rhs=ident_f32[:], start=True, stop=True)
+        rstd_ps = psum.tile([P, D], F32, tag="h2")
+        nc.tensor.matmul(out=rstd_ps[:], lhsT=z_rstd[:].to_broadcast([P, P]), rhs=ident_f32[:], start=True, stop=True)
+        zx_rows = keep.tile([P, ROW_TILES, D], F32)
+        nc.vector.tensor_tensor(
+            out=zx_rows[:], in0=z_rows[:], in1=mean_ps[:].unsqueeze(1).to_broadcast([P, ROW_TILES, D]), op=ALU.subtract
         )
-
-        for index, (result_t, out) in enumerate(((z_t, out_0), (zx_t, out_1))):
-            back_ps = psum.tile([P, ROW_TILES, D], F32, name="back_ps%d" % index, tag="h%d" % index)
-            for r in range(ROW_TILES):
-                nc.tensor.transpose(back_ps[:, r, :], result_t[:, r * P : (r + 1) * P], ident_f32[:])
-            result = keep.tile([P, ROW_TILES, D], F32, name="result%d" % index)
-            nc.scalar.copy(out=result[:], in_=back_ps[:])
-            nc.sync.dma_start(out=out.rearrange("(r p) d -> p r d", p=P), in_=result[:])
+        nc.vector.tensor_tensor(
+            out=zx_rows[:], in0=zx_rows[:], in1=rstd_ps[:].unsqueeze(1).to_broadcast([P, ROW_TILES, D]), op=ALU.mult
+        )
+        nc.sync.dma_start(out=out_1.rearrange("(r p) d -> p r d", p=P), in_=zx_rows[:])

@@ -22,8 +22,6 @@ ROW_TILES = ROWS // P
 PASSES_1 = EN1 // K_PASS
 BN_EPS = 1e-5
 
-HALF = EN2 // 2
-
 VECTOR_COLS = 64
 VECTOR_ROWS = 168
 
@@ -87,9 +85,8 @@ def tile_modelvd_pa_s_kernel(tc, en1, W2, b2, Wmean, Wlogvar, eps, out_0, out_1)
                 for u in range(2):
                     nc.tensor.transpose(x_t[:, g, u, :], words[:, g, u, :], ident_f32[:])
             grouped_words = x_grouped[:].bitcast(F32).rearrange("p g (r u) -> p g r u", u=2)
-            nc.scalar.copy(
-                out=grouped_words[:, :, r * P : (r + 1) * P, :], in_=x_t[:].rearrange("p g u r -> p g r u")
-            )
+            copy_out = nc.vector.tensor_copy if r == 0 else nc.scalar.copy
+            copy_out(out=grouped_words[:, :, r * P : (r + 1) * P, :], in_=x_t[:].rearrange("p g u r -> p g r u"))
 
         def quantise_x(r):
             for g in range(PASSES_1):
@@ -110,12 +107,13 @@ def tile_modelvd_pa_s_kernel(tc, en1, W2, b2, Wmean, Wlogvar, eps, out_0, out_1)
             nc.vector.tensor_copy(out=dst[:, :VECTOR_COLS, :, blocks], in_=src[:, :VECTOR_COLS, :, blocks])
             nc.scalar.copy(out=dst[:, VECTOR_COLS:, :, blocks], in_=src[:, VECTOR_COLS:, :, blocks])
 
-        def quantise_w(g, half):
-            nc.vector.quantize_mx(
-                out=w_codes[g][:, half * HALF : (half + 1) * HALF].bitcast(FP8X4),
-                scales=w_scales[g][:, half * HALF : (half + 1) * HALF],
-                in_=w_grouped[g][:, half * HALF * PACK : (half + 1) * HALF * PACK],
-            )
+        def quantise_w(g):
+            for j in range(PACK):
+                nc.vector.quantize_mx(
+                    out=w_codes[g][:, j * P : (j + 1) * P].bitcast(FP8X4),
+                    scales=w_scales[g][:, j * P : (j + 1) * P],
+                    in_=w_grouped[g][:, j * P * PACK : (j + 1) * P * PACK],
+                )
 
         h_ps = [psum.tile([P, ROWS], F32, name="h_ps%d" % j, tag="h%d" % j) for j in range(PACK)]
 
@@ -136,14 +134,12 @@ def tile_modelvd_pa_s_kernel(tc, en1, W2, b2, Wmean, Wlogvar, eps, out_0, out_1)
         regroup_w(0, 0)
         regroup_w(0, 1)
         quantise_x(0)
-        quantise_w(0, 0)
-        quantise_w(0, 1)
         quantise_x(1)
+        quantise_w(0)
         multiply_1(0)
         regroup_w(1, 0)
         regroup_w(1, 1)
-        quantise_w(1, 0)
-        quantise_w(1, 1)
+        quantise_w(1)
         multiply_1(1)
 
         head_grouped = keep.tile([P, 2 * D * PACK], BF16, align_bytes=64)

@@ -45,6 +45,10 @@ def tile_modelvd_pa_s_kernel(tc, en1, W2, b2, Wmean, Wlogvar, eps, out_0, out_1)
         nc.vector.memset(bn_eps[:], BN_EPS)
         one = keep.tile([P, 1], F32)
         nc.vector.memset(one[:], 1.0)
+        stats = [keep.tile([P, 9], F32, name="stats%d" % w) for w in range(2)]
+        for w in range(2):
+            nc.vector.memset(stats[w][:, 6:8], 0.0)
+            nc.vector.memset(stats[w][:, 8:9], ROWS * BN_EPS)
 
         x_sb = [keep.tile([P, EN1], BF16, name="x_sb%d" % r) for r in range(ROW_TILES)]
         w_raw = [keep.tile([P, PACK, EN2], BF16, name="w_raw%d" % g) for g in range(PASSES_1)]
@@ -166,10 +170,10 @@ def tile_modelvd_pa_s_kernel(tc, en1, W2, b2, Wmean, Wlogvar, eps, out_0, out_1)
         h_grouped = keep.tile([P, ROWS * PACK], BF16, align_bytes=64)
         h_codes = keep.tile([P, ROWS], U32, align_bytes=64)
         h_scales = keep.tile([P, ROWS], U8, align_bytes=64)
-        h_dst = h_grouped[:].rearrange("p (r t) -> p r t", t=PACK)
-        h_src = h_bf[:].rearrange("p t r -> p r t")
-        nc.vector.tensor_copy(out=h_dst[:, :VECTOR_ROWS], in_=h_src[:, :VECTOR_ROWS])
-        nc.scalar.copy(out=h_dst[:, VECTOR_ROWS:], in_=h_src[:, VECTOR_ROWS:])
+        h_dst = h_grouped[:].rearrange("p (c i t) -> p c t i", i=4, t=PACK)
+        h_src = h_bf[:].rearrange("p t (c i) -> p c t i", i=4)
+        nc.vector.tensor_copy(out=h_dst[:, : VECTOR_ROWS // 4], in_=h_src[:, : VECTOR_ROWS // 4])
+        nc.scalar.copy(out=h_dst[:, VECTOR_ROWS // 4 :], in_=h_src[:, VECTOR_ROWS // 4 :])
         nc.vector.quantize_mx(out=h_codes[:].bitcast(FP8X4), scales=h_scales[:], in_=h_grouped[:])
 
         head_ps = [psum.tile([P, ROWS], F32, name="head_ps%d" % w, tag="early%d" % w) for w in range(2)]
@@ -186,16 +190,13 @@ def tile_modelvd_pa_s_kernel(tc, en1, W2, b2, Wmean, Wlogvar, eps, out_0, out_1)
         lv_ps, m_ps = head_ps
 
         mean_var = [keep.tile([P, 2], F32, name="mean_var%d" % w) for w in range(2)]
-        var_eps = [keep.tile([P, 1], F32, name="var_eps%d" % w) for w in range(2)]
         rstd = [keep.tile([P, 1], F32, name="rstd%d" % w) for w in range(2)]
-        stats = [keep.tile([P, 6], F32, name="stats%d" % w) for w in range(2)]
         for w in range(2):
-            nc.vector.bn_stats(out=stats[w][:], in_=head_ps[w][:])
+            nc.vector.bn_stats(out=stats[w][:, 0:6], in_=head_ps[w][:])
         for w in range(2):
             nc.vector.bn_aggr(out=mean_var[w][:], in_=stats[w][:])
         for w in range(2):
-            nc.vector.tensor_scalar_add(out=var_eps[w][:], in0=mean_var[w][:, 1:2], scalar1=BN_EPS)
-            nc.gpsimd.tensor_tensor(out=rstd[w][:], in0=var_eps[w][:], in1=neg_half[:], op=ALU.pow)
+            nc.gpsimd.tensor_tensor(out=rstd[w][:], in0=mean_var[w][:, 1:2], in1=neg_half[:], op=ALU.pow)
         lv_half = keep.tile([P, ROWS], F32)
         nc.vector.tensor_scalar(
             out=lv_half[:], in0=lv_ps[:], scalar1=mean_var[0][:, 0:1], scalar2=0.5, op0=ALU.subtract, op1=ALU.mult
@@ -226,9 +227,9 @@ def tile_modelvd_pa_s_kernel(tc, en1, W2, b2, Wmean, Wlogvar, eps, out_0, out_1)
         z_rstd = keep.tile([P, 1], F32)
         nc.scalar.activation(out=z_rstd[:], in_=z_mean_var[:, 1:2], func=ACT.Abs_reciprocal_sqrt, bias=bn_eps[:])
         mean_ps = psum.tile([P, D], F32, tag="h1")
-        nc.tensor.matmul(out=mean_ps[:], lhsT=z_mean_var[:, 0:1].to_broadcast([P, P]), rhs=ident_f32[:], start=True, stop=True)
+        nc.tensor.transpose(mean_ps[:], z_mean_var[:, 0:1].to_broadcast([P, P]), ident_f32[:])
         rstd_ps = psum.tile([P, D], F32, tag="h2")
-        nc.tensor.matmul(out=rstd_ps[:], lhsT=z_rstd[:].to_broadcast([P, P]), rhs=ident_f32[:], start=True, stop=True)
+        nc.tensor.transpose(rstd_ps[:], z_rstd[:].to_broadcast([P, P]), ident_f32[:])
         zx_rows = keep.tile([P, ROW_TILES, D], F32)
         nc.vector.tensor_tensor(
             out=zx_rows[:], in0=z_rows[:], in1=mean_ps[:].unsqueeze(1).to_broadcast([P, ROW_TILES, D]), op=ALU.subtract

@@ -22,7 +22,7 @@ ROW_TILES = ROWS // P
 PASSES_1 = EN1 // K_PASS
 BN_EPS = 1e-5
 
-VECTOR_COLS = 64
+VECTOR_COLS = (84, 64)
 VECTOR_ROWS = 168
 
 FLOPS = 2 * ROWS * EN1 * EN2 + 2 * 2 * ROWS * EN2 * D
@@ -66,13 +66,13 @@ def tile_modelvd_pa_s_kernel(tc, en1, W2, b2, Wmean, Wlogvar, eps, out_0, out_1)
         load_x(1)
         load_w(0)
         load_w(1)
+        b2_bf = keep.tile([P, PACK], BF16)
+        nc.sync.dma_start(out=b2_bf[:], in_=b2.rearrange("(p j) -> p j", j=PACK))
         head_raw = keep.tile([P, 2, PACK, D], BF16)
         nc.sync.dma_start(out=head_raw[:, 0], in_=Wlogvar.rearrange("(p t) d -> p t d", t=PACK))
         nc.sync.dma_start(out=head_raw[:, 1], in_=Wmean.rearrange("(p t) d -> p t d", t=PACK))
         eps_sb = keep.tile([P, ROW_TILES, D], BF16)
         nc.sync.dma_start(out=eps_sb[:], in_=eps.rearrange("(r p) d -> p r d", p=P))
-        b2_bf = keep.tile([P, PACK], BF16)
-        nc.scalar.dma_start(out=b2_bf[:], in_=b2.rearrange("(p j) -> p j", j=PACK))
         b2_f32 = keep.tile([P, PACK], F32)
         nc.gpsimd.tensor_copy(out=b2_f32[:], in_=b2_bf[:])
         warm = keep.tile([P, 1], F32)
@@ -108,8 +108,9 @@ def tile_modelvd_pa_s_kernel(tc, en1, W2, b2, Wmean, Wlogvar, eps, out_0, out_1)
             blocks = slice(2 * half, 2 * half + 2)
             dst = w_grouped[g][:].rearrange("p (j m t) -> p m t j", j=PACK, t=PACK)
             src = w_raw[g][:].rearrange("p t (m j) -> p m t j", j=PACK)
-            nc.vector.tensor_copy(out=dst[:, :VECTOR_COLS, :, blocks], in_=src[:, :VECTOR_COLS, :, blocks])
-            nc.scalar.copy(out=dst[:, VECTOR_COLS:, :, blocks], in_=src[:, VECTOR_COLS:, :, blocks])
+            cut = VECTOR_COLS[g]
+            nc.vector.tensor_copy(out=dst[:, :cut, :, blocks], in_=src[:, :cut, :, blocks])
+            nc.scalar.copy(out=dst[:, cut:, :, blocks], in_=src[:, cut:, :, blocks])
 
         def quantise_w(g):
             for j in range(PACK):

from contextlib import ExitStack

import concourse.mybir as mybir
from concourse.masks import make_identity

F32 = mybir.dt.float32
BF16 = mybir.dt.bfloat16
U32 = mybir.dt.uint32
U8 = mybir.dt.uint8
FP8X4 = mybir.dt.float8_e4m3fn_x4
ALU = mybir.AluOpType
ACT = mybir.ActivationFunctionType

P = 128
PACK = 4
K_PASS = P * PACK
ROWS = 256
EN1 = 1024
EN2 = 512
D = 128
ROW_TILES = ROWS // P
PASSES_1 = EN1 // K_PASS
BN_EPS = 1e-5

VECTOR_COLS = (84, 64)
VECTOR_ROWS = 168

FLOPS = 2 * ROWS * EN1 * EN2 + 2 * 2 * ROWS * EN2 * D


def tile_modelvd_pa_s_kernel(tc, en1, W2, b2, Wmean, Wlogvar, eps, out_0, out_1):
    nc = tc.nc
    with ExitStack() as stack:
        keep = stack.enter_context(tc.tile_pool(name="keep", bufs=1))
        psum = stack.enter_context(tc.psum_pool(name="psum", bufs=1))
        stack.enter_context(tc.manual_schedule())

        ident_f32 = keep.tile([P, P], F32)
        make_identity(nc, ident_f32[:])
        ident_bf16 = keep.tile([P, P], BF16)
        make_identity(nc, ident_bf16[:])
        neg_half = keep.tile([P, 1], F32)
        nc.vector.memset(neg_half[:], -0.5)
        bn_eps = keep.tile([P, 1], F32)
        nc.vector.memset(bn_eps[:], BN_EPS)
        one = keep.tile([P, 1], F32)
        nc.vector.memset(one[:], 1.0)
        stats = [keep.tile([P, 9], F32, name="stats%d" % w) for w in range(2)]
        for w in range(2):
            nc.vector.memset(stats[w][:, 6:8], 0.0)
            nc.vector.memset(stats[w][:, 8:9], ROWS * BN_EPS)

        x_sb = [keep.tile([P, EN1], BF16, name="x_sb%d" % r) for r in range(ROW_TILES)]
        w_raw = [keep.tile([P, PACK, EN2], BF16, name="w_raw%d" % g) for g in range(PASSES_1)]

        def load_x(r):
            nc.sync.dma_start(out=x_sb[r][:], in_=en1[r * P : (r + 1) * P, :])

        def load_w(g):
            nc.sync.dma_start(
                out=w_raw[g][:].rearrange("p (u e) n -> p u (e n)", u=2),
                in_=W2[g * K_PASS : (g + 1) * K_PASS, :].rearrange("(u p e) n -> p u (e n)", u=2, e=2),
            )

        load_x(0)
        load_x(1)
        load_w(0)
        load_w(1)
        b2_bf = keep.tile([P, PACK], BF16)
        nc.sync.dma_start(out=b2_bf[:], in_=b2.rearrange("(p j) -> p j", j=PACK))
        head_raw = keep.tile([P, 2, PACK, D], BF16)
        nc.sync.dma_start(out=head_raw[:, 0], in_=Wlogvar.rearrange("(p t) d -> p t d", t=PACK))
        nc.sync.dma_start(out=head_raw[:, 1], in_=Wmean.rearrange("(p t) d -> p t d", t=PACK))
        eps_sb = keep.tile([P, ROW_TILES, D], BF16)
        nc.sync.dma_start(out=eps_sb[:], in_=eps.rearrange("(r p) d -> p r d", p=P))
        b2_f32 = keep.tile([P, PACK], F32)
        nc.gpsimd.tensor_copy(out=b2_f32[:], in_=b2_bf[:])
        warm = keep.tile([P, 1], F32)
        nc.scalar.activation(out=warm[:], in_=one[:], func=ACT.Exp)

        x_grouped = keep.tile([P, PASSES_1, ROWS * PACK], BF16, align_bytes=64)
        x_codes = keep.tile([P, PASSES_1, ROWS], U32, align_bytes=64)
        x_scales = keep.tile([P, PASSES_1, ROWS], U8, align_bytes=64)

        def transpose_x(r):
            x_t = psum.tile([P, PASSES_1, 2, P], F32, name="x_t%d" % r, tag="early%d" % r)
            words = x_sb[r][:].bitcast(F32).rearrange("p (g u w) -> p g u w", g=PASSES_1, u=2)
            for g in range(PASSES_1):
                for u in range(2):
                    nc.tensor.transpose(x_t[:, g, u, :], words[:, g, u, :], ident_f32[:])
            grouped_words = x_grouped[:].bitcast(F32).rearrange("p g (r u) -> p g r u", u=2)
            copy_out = nc.vector.tensor_copy if r == 0 else nc.scalar.copy
            copy_out(out=grouped_words[:, :, r * P : (r + 1) * P, :], in_=x_t[:].rearrange("p g u r -> p g r u"))

        def quantise_x(r):
            for g in range(PASSES_1):
                nc.vector.quantize_mx(
                    out=x_codes[:, g, r * P : (r + 1) * P].bitcast(FP8X4),
                    scales=x_scales[:, g, r * P : (r + 1) * P],
                    in_=x_grouped[:, g, r * P * PACK : (r + 1) * P * PACK],
                )

        w_grouped = [keep.tile([P, EN2 * PACK], BF16, name="w_grouped%d" % g, align_bytes=64) for g in range(PASSES_1)]
        w_codes = [keep.tile([P, EN2], U32, name="w_codes%d" % g, align_bytes=64) for g in range(PASSES_1)]
        w_scales = [keep.tile([P, EN2], U8, name="w_scales%d" % g, align_bytes=64) for g in range(PASSES_1)]

        def regroup_w(g, half):
            blocks = slice(2 * half, 2 * half + 2)
            dst = w_grouped[g][:].rearrange("p (j m t) -> p m t j", j=PACK, t=PACK)
            src = w_raw[g][:].rearrange("p t (m j) -> p m t j", j=PACK)
            cut = VECTOR_COLS[g]
            nc.vector.tensor_copy(out=dst[:, :cut, :, blocks], in_=src[:, :cut, :, blocks])
            nc.scalar.copy(out=dst[:, cut:, :, blocks], in_=src[:, cut:, :, blocks])

        def quantise_w(g):
            for j in range(PACK):
                nc.vector.quantize_mx(
                    out=w_codes[g][:, j * P : (j + 1) * P].bitcast(FP8X4),
                    scales=w_scales[g][:, j * P : (j + 1) * P],
                    in_=w_grouped[g][:, j * P * PACK : (j + 1) * P * PACK],
                )

        h_ps = [psum.tile([P, ROWS], F32, name="h_ps%d" % j, tag="h%d" % j) for j in range(PACK)]

        def multiply_1(g):
            for j in range(PACK):
                nc.tensor.matmul_mx(
                    out=h_ps[j][:],
                    lhsT=w_codes[g][:, j * P : (j + 1) * P].bitcast(FP8X4),
                    lhsT_scale=w_scales[g][:, j * P : (j + 1) * P],
                    rhs=x_codes[:, g, :].bitcast(FP8X4),
                    rhs_scale=x_scales[:, g, :],
                    start=(g == 0),
                    stop=(g == PASSES_1 - 1),
                )

        transpose_x(0)
        transpose_x(1)
        regroup_w(0, 0)
        regroup_w(0, 1)
        quantise_x(0)
        quantise_x(1)
        quantise_w(0)
        multiply_1(0)
        regroup_w(1, 0)
        regroup_w(1, 1)
        quantise_w(1)
        multiply_1(1)

        head_grouped = keep.tile([P, 2 * D * PACK], BF16, align_bytes=64)
        head_codes = keep.tile([P, 2 * D], U32, align_bytes=64)
        head_scales = keep.tile([P, 2 * D], U8, align_bytes=64)
        head_dst = head_grouped[:].rearrange("p (w d t) -> p w d t", w=2, t=PACK)
        head_src = head_raw[:].rearrange("p w t d -> p w d t")
        nc.vector.tensor_copy(out=head_dst[:, 0], in_=head_src[:, 0])
        nc.scalar.copy(out=head_dst[:, 1], in_=head_src[:, 1])
        nc.vector.quantize_mx(out=head_codes[:].bitcast(FP8X4), scales=head_scales[:], in_=head_grouped[:])
        eps_t = psum.tile([P, ROWS], BF16, tag="eps")
        for r in range(ROW_TILES):
            nc.tensor.transpose(eps_t[:, r * P : (r + 1) * P], eps_sb[:, r, :], ident_bf16[:])

        h_bf = keep.tile([P, PACK, ROWS], BF16)
        for j in range(PACK):
            if j % 2 == 0:
                nc.scalar.activation(out=h_bf[:, j, :], in_=h_ps[j][:], func=ACT.Relu, bias=b2_f32[:, j : j + 1])
            else:
                nc.vector.tensor_scalar(
                    out=h_bf[:, j, :], in0=h_ps[j][:], scalar1=b2_f32[:, j : j + 1], scalar2=0.0,
                    op0=ALU.add, op1=ALU.max,
                )
        h_grouped = keep.tile([P, ROWS * PACK], BF16, align_bytes=64)
        h_codes = keep.tile([P, ROWS], U32, align_bytes=64)
        h_scales = keep.tile([P, ROWS], U8, align_bytes=64)
        h_dst = h_grouped[:].rearrange("p (c i t) -> p c t i", i=4, t=PACK)
        h_src = h_bf[:].rearrange("p t (c i) -> p c t i", i=4)
        nc.vector.tensor_copy(out=h_dst[:, : VECTOR_ROWS // 4], in_=h_src[:, : VECTOR_ROWS // 4])
        nc.scalar.copy(out=h_dst[:, VECTOR_ROWS // 4 :], in_=h_src[:, VECTOR_ROWS // 4 :])
        nc.vector.quantize_mx(out=h_codes[:].bitcast(FP8X4), scales=h_scales[:], in_=h_grouped[:])

        head_ps = [psum.tile([P, ROWS], F32, name="head_ps%d" % w, tag="early%d" % w) for w in range(2)]
        for w in range(2):
            nc.tensor.matmul_mx(
                out=head_ps[w][:],
                lhsT=head_codes[:, w * D : (w + 1) * D].bitcast(FP8X4),
                lhsT_scale=head_scales[:, w * D : (w + 1) * D],
                rhs=h_codes[:].bitcast(FP8X4),
                rhs_scale=h_scales[:],
                start=True,
                stop=True,
            )
        lv_ps, m_ps = head_ps

        mean_var = [keep.tile([P, 2], F32, name="mean_var%d" % w) for w in range(2)]
        rstd = [keep.tile([P, 1], F32, name="rstd%d" % w) for w in range(2)]
        for w in range(2):
            nc.vector.bn_stats(out=stats[w][:, 0:6], in_=head_ps[w][:])
        for w in range(2):
            nc.vector.bn_aggr(out=mean_var[w][:], in_=stats[w][:])
        for w in range(2):
            nc.gpsimd.tensor_tensor(out=rstd[w][:], in0=mean_var[w][:, 1:2], in1=neg_half[:], op=ALU.pow)
        lv_half = keep.tile([P, ROWS], F32)
        nc.vector.tensor_scalar(
            out=lv_half[:], in0=lv_ps[:], scalar1=mean_var[0][:, 0:1], scalar2=0.5, op0=ALU.subtract, op1=ALU.mult
        )
        m_centred = keep.tile([P, ROWS], F32)
        nc.vector.tensor_scalar_sub(out=m_centred[:], in0=m_ps[:], scalar1=mean_var[1][:, 0:1])
        std_dev = keep.tile([P, ROWS], F32)
        nc.scalar.activation(out=std_dev[:], in_=lv_half[:], func=ACT.Exp, scale=rstd[0][:])
        nc.scalar.activation(out=warm[:], in_=one[:], func=ACT.Abs_reciprocal_sqrt)
        noise = keep.tile([P, ROWS], F32)
        nc.vector.tensor_tensor(out=noise[:], in0=std_dev[:], in1=eps_t[:], op=ALU.mult)
        z_t = keep.tile([P, ROWS], F32)
        nc.vector.scalar_tensor_tensor(
            out=z_t[:], in0=m_centred[:], scalar=rstd[1][:], in1=noise[:], op0=ALU.mult, op1=ALU.add
        )

        z_ps = psum.tile([P, ROW_TILES, D], F32, tag="h0")
        for r in range(ROW_TILES):
            nc.tensor.transpose(z_ps[:, r, :], z_t[:, r * P : (r + 1) * P], ident_f32[:])
        z_rows = keep.tile([P, ROW_TILES, D], F32)
        nc.scalar.copy(out=z_rows[:], in_=z_ps[:])
        nc.sync.dma_start(out=out_0.rearrange("(r p) d -> p r d", p=P), in_=z_rows[:])

        z_mean_var = keep.tile([P, 2], F32)
        z_stats = keep.tile([P, 6], F32)
        nc.vector.bn_stats(out=z_stats[:], in_=z_t[:])
        nc.vector.bn_aggr(out=z_mean_var[:], in_=z_stats[:])
        z_rstd = keep.tile([P, 1], F32)
        nc.scalar.activation(out=z_rstd[:], in_=z_mean_var[:, 1:2], func=ACT.Abs_reciprocal_sqrt, bias=bn_eps[:])
        mean_ps = psum.tile([P, D], F32, tag="h1")
        nc.tensor.transpose(mean_ps[:], z_mean_var[:, 0:1].to_broadcast([P, P]), ident_f32[:])
        rstd_ps = psum.tile([P, D], F32, tag="h2")
        nc.tensor.transpose(rstd_ps[:], z_rstd[:].to_broadcast([P, P]), ident_f32[:])
        zx_rows = keep.tile([P, ROW_TILES, D], F32)
        nc.vector.tensor_tensor(
            out=zx_rows[:], in0=z_rows[:], in1=mean_ps[:].unsqueeze(1).to_broadcast([P, ROW_TILES, D]), op=ALU.subtract
        )
        nc.vector.tensor_tensor(
            out=zx_rows[:], in0=zx_rows[:], in1=rstd_ps[:].unsqueeze(1).to_broadcast([P, ROW_TILES, D]), op=ALU.mult
        )
        nc.sync.dma_start(out=out_1.rearrange("(r p) d -> p r d", p=P), in_=zx_rows[:])
